import numpy as np
import ml_dtypes


def mxq(x, axis, fmt="e4m3"):
    dtype, down = {"e4m3": (ml_dtypes.float8_e4m3fn, 7), "e5m2": (ml_dtypes.float8_e5m2, 14)}[fmt]
    v = np.moveaxis(np.asarray(x, np.float32).astype(ml_dtypes.bfloat16).astype(np.float64), axis, -1)
    blocks = v.reshape(v.shape[:-1] + (-1, 32))
    amax = np.abs(blocks).max(-1, keepdims=True)
    byte = np.maximum(np.where(amax > 0, np.frexp(amax)[1] - 1 + 127, 0) - down, 1)
    scale = np.exp2(byte - 127.0)
    codes = (blocks / scale).astype(np.float32).astype(dtype).astype(np.float64)
    return np.moveaxis((codes * scale).reshape(v.shape), -1, axis)


WIDE = False


def mx_kscale(k):
    if not WIDE:
        return np.ones(k)
    levels = np.array([10, -10, 5, -5, 0])
    a = np.random.permutation(np.resize(levels, k // 512 * 4)).reshape(k // 512, 4)
    idx = np.arange(k)
    return np.exp2(a[idx // 512, idx % 128 // 32])


BF16 = ml_dtypes.bfloat16


def bf(x):
    return np.asarray(x, np.float32).astype(BF16)


def f64(x):
    return np.asarray(x).astype(np.float64)


B, I, O, G, P = 16384, 128, 256, 5, 3
NC = G + P
KN = G // 2


def extend_grid(grid, k):
    h = (grid[:, -1:] - grid[:, :1]) / (grid.shape[1] - 1)
    for _ in range(k):
        grid = np.concatenate([grid[:, :1] - h, grid, grid[:, -1:] + h], axis=1)
    return grid


def b_batch(x, grid, k):
    g = extend_grid(grid, k)[None, :, :]
    xe = x[..., None]
    bases = np.where((xe >= g[..., :-1]) & (xe < g[..., 1:]), 1.0, 0.0)
    eps = 1e-8
    for order in range(1, k + 1):
        d1 = g[..., order:-1] - g[..., :-(order + 1)]
        d2 = g[..., order + 1:] - g[..., 1:-order]
        t1 = (xe - g[..., :-(order + 1)]) / np.where(d1 == 0, eps, d1) * bases[..., :-1]
        t2 = (g[..., order + 1:] - xe) / np.where(d2 == 0, eps, d2) * bases[..., 1:]
        bases = t1 + t2
    return np.nan_to_num(bases)


def setup_inputs():
    knots = bf(np.linspace(-1.0, 1.0, G + 1)[None, :] + (np.random.random((I, G + 1)) * 2.0 - 1.0) * 0.15 * (2.0 / G))
    mid = f64(knots)[None, :, KN]
    t = np.repeat(mx_kscale(NC * I)[:I:32], 32)
    r = np.exp2(-np.round(0.7 * np.abs(np.log2(t))))
    x = mid + r[None, :] * (np.random.random((B, I)) * 2.0 - 1.0 - mid)
    coef = np.random.standard_normal((I, O, NC)) * 1.5 / np.sqrt(I)
    coef[:, :, KN - 1] /= (r ** P)[:, None]
    coef[:, :, KN + P] /= (r ** P)[:, None]
    return {"x": bf(x),
            "grid": knots,
            "coef": bf(coef),
            "base_weight": bf(np.random.standard_normal((I, O)) * 1.7 / np.sqrt(I)),
            "base_bias": bf(np.random.standard_normal(O) * 0.3)}


def reference(x, grid, coef, base_weight, base_bias):
    x = f64(x)
    bases = b_batch(x, f64(grid), P)
    bq = mxq(bases.transpose(0, 2, 1).reshape(B, NC * I), 1, "e4m3")
    cq = mxq(f64(coef).transpose(2, 0, 1).reshape(NC * I, O), 0, "e4m3")
    spline_sum = bq @ cq
    base_val = x @ f64(base_weight) + f64(base_bias)
    return base_val + spline_sum

@@ -1,0 +1,247 @@
+import concourse.mybir as mybir
+from concourse.masks import make_identity
+
+F32 = mybir.dt.float32
+BF16 = mybir.dt.bfloat16
+U32 = mybir.dt.uint32
+U8 = mybir.dt.uint8
+I32 = mybir.dt.int32
+FP8X4 = mybir.dt.float8_e4m3fn_x4
+ALU = mybir.AluOpType
+AF = mybir.ActivationFunctionType
+
+B, I, O, NC = 16384, 128, 256, 8
+FLOPS = 2 * B * (NC * I + I) * O
+P = 128
+ROWS = B // P
+SUP = 4
+CH_ROWS = 4 * SUP
+NCH = ROWS // CH_ROWS
+W = SUP * P
+NKN = 12
+ACT_REGROUP = (0, 1, 2, 3, 4, 5, 6)
+
+
+def tile_kanlinear_t_kernel(tc, x, grid, coef, base_weight, base_bias, out):
+    nc = tc.nc
+    xv = x.rearrange("(n r) i -> n r i", r=ROWS)
+    ov = out.rearrange("(n r) o -> n r o", r=ROWS)
+    with tc.tile_pool(name="const", bufs=1) as const:
+        ident_f = const.tile([P, P], F32)
+        make_identity(nc, ident_f[:])
+        ident_b = const.tile([P, P], BF16)
+        make_identity(nc, ident_b[:])
+        kn = const.tile([P, 4, NKN], F32)
+        nk = const.tile([P, 4, NKN], F32)
+        a0 = const.tile([P, 4, NC], F32)
+        a1 = const.tile([P, 4, NC], F32)
+        nb4 = const.tile([P, 4, NC], F32)
+        nb3 = const.tile([P, 4, NC], F32)
+        bw = const.tile([P, O], BF16)
+        bias2 = const.tile([P, 2, O], F32)
+        rh = const.tile([P, NC, 2, 2 * O], U32, align_bytes=64)
+        rhs_sc = const.tile([P, NC, 2, 2 * O], U8, align_bytes=64)
+
+        with tc.tile_pool(name="prep", bufs=1) as prep:
+            g_bf = prep.tile([P, 24], BF16)
+            gsrc = grid.rearrange("(j t) g -> j (t g)", t=4)
+            for r in range(4):
+                nc.sync.dma_start(out=g_bf[32 * r : 32 * r + 32, :], in_=gsrc)
+            nc.scalar.dma_start(out=bw[:], in_=base_weight)
+            bias_bf = prep.tile([P, O], BF16)
+            nc.scalar.dma_start(out=bias_bf[:], in_=base_bias.partition_broadcast(P))
+            craw = prep.tile([P, 4 * O * NC], BF16)
+            csrc = coef.rearrange("(j t) o k -> j (t o k)", t=4)
+            for r in range(4):
+                nc.scalar.dma_start(out=craw[32 * r : 32 * r + 32, :], in_=csrc)
+
+            nc.vector.tensor_copy(out=kn[:, :, 3:9], in_=g_bf[:].rearrange("p (t g) -> p t g", g=6))
+            five = prep.tile([P, 1], F32)
+            nc.vector.memset(five[:], 5.0)
+            fifth = prep.tile([P, 1], F32)
+            nc.vector.reciprocal(out=fifth[:], in_=five[:])
+            hh = prep.tile([P, 4, 1], F32)
+            nc.vector.tensor_tensor(out=hh[:], in0=kn[:, :, 8:9], in1=kn[:, :, 3:4], op=ALU.subtract)
+            nc.vector.tensor_scalar(out=hh[:], in0=hh[:], scalar1=fifth[:, 0:1], scalar2=None, op0=ALU.mult)
+            for m in (2, 1, 0):
+                nc.vector.tensor_tensor(out=kn[:, :, m : m + 1], in0=kn[:, :, m + 1 : m + 2], in1=hh[:], op=ALU.subtract)
+            for m in (9, 10, 11):
+                nc.vector.tensor_tensor(out=kn[:, :, m : m + 1], in0=kn[:, :, m - 1 : m], in1=hh[:], op=ALU.add)
+            nc.vector.tensor_scalar(out=nk[:], in0=kn[:], scalar1=-1.0, scalar2=None, op0=ALU.mult)
+            d1 = prep.tile([P, 4, 11], F32)
+            d2 = prep.tile([P, 4, 10], F32)
+            d3 = prep.tile([P, 4, 9], F32)
+            d4 = prep.tile([P, 4, 8], F32)
+            nc.vector.tensor_tensor(out=d1[:], in0=kn[:, :, 1:12], in1=kn[:, :, 0:11], op=ALU.subtract)
+            nc.vector.tensor_tensor(out=d2[:], in0=kn[:, :, 2:12], in1=kn[:, :, 0:10], op=ALU.subtract)
+            nc.vector.tensor_tensor(out=d3[:], in0=kn[:, :, 3:12], in1=kn[:, :, 0:9], op=ALU.subtract)
+            nc.vector.tensor_tensor(out=d4[:], in0=kn[:, :, 4:12], in1=kn[:, :, 0:8], op=ALU.subtract)
+
+            def product(dst, factors):
+                nc.vector.tensor_tensor(out=dst[:], in0=factors[0], in1=factors[1], op=ALU.mult)
+                for f in factors[2:]:
+                    nc.vector.tensor_tensor(out=dst[:], in0=dst[:], in1=f, op=ALU.mult)
+
+            den0 = prep.tile([P, 4, NC], F32)
+            product(den0, [d1[:, :, 0:8], d2[:, :, 0:8], d3[:, :, 0:8]])
+            nc.vector.reciprocal(out=a0[:], in_=den0[:])
+            den1 = prep.tile([P, 4, NC], F32)
+            product(den1, [d1[:, :, 0:8], d1[:, :, 1:9], d2[:, :, 1:9], d3[:, :, 1:9]])
+            nc.vector.reciprocal(out=den1[:], in_=den1[:])
+            nc.vector.tensor_tensor(out=a1[:], in0=den1[:], in1=d4[:], op=ALU.mult)
+            den4 = prep.tile([P, 4, NC], F32)
+            product(den4, [d3[:, :, 1:9], d2[:, :, 2:10], d1[:, :, 3:11]])
+            nc.vector.reciprocal(out=den4[:], in_=den4[:])
+            nc.vector.tensor_scalar(out=nb4[:], in0=den4[:], scalar1=-1.0, scalar2=None, op0=ALU.mult)
+            den3 = prep.tile([P, 4, NC], F32)
+            product(den3, [d3[:, :, 0:8], d2[:, :, 1:9], d1[:, :, 2:10], d1[:, :, 3:11]])
+            nc.vector.reciprocal(out=den3[:], in_=den3[:])
+            nc.vector.tensor_tensor(out=den3[:], in0=den3[:], in1=d4[:], op=ALU.mult)
+            nc.vector.tensor_scalar(out=nb3[:], in0=den3[:], scalar1=-1.0, scalar2=None, op0=ALU.mult)
+
+            for h in range(2):
+                nc.vector.tensor_copy(out=bias2[:, h, :], in_=bias_bf[:])
+
+            def prepare_coef():
+                nc.vector.memset(rh[:].rearrange("p k q w -> p (k q w)").bitcast(I32), 0)
+                nc.vector.memset(rhs_sc[:].rearrange("p k q w -> p (k q w)").bitcast(I32), 0)
+                cv = craw[:].rearrange("p (t o k) -> p t o k", t=4, o=O, k=NC)
+                call = prep.tile([P, NC, O], U32, align_bytes=64)
+                sall = prep.tile([P, NC, O], U8, align_bytes=64)
+                for k in range(NC):
+                    cg = prep.tile([P, O, 4], BF16, align_bytes=64, tag="cg", bufs=2)
+                    nc.scalar.copy(out=cg[:], in_=cv[:, :, :, k].rearrange("p t o -> p o t"))
+                    nc.vector.quantize_mx(
+                        out=call[:, k, :].bitcast(FP8X4),
+                        scales=sall[:, k, :],
+                        in_=cg[:].rearrange("p o t -> p (o t)"),
+                    )
+                for r in range(4):
+                    q, h = r // 2, r % 2
+                    rows = slice(32 * r, 32 * r + 32)
+                    nc.vector.tensor_copy(
+                        out=rh[rows, :, q, h * O : (h + 1) * O].bitcast(I32),
+                        in_=call[rows, :, :].bitcast(I32),
+                    )
+                    nc.vector.tensor_copy(
+                        out=rhs_sc[rows, :, q, h * O : (h + 1) * O].bitcast(I32),
+                        in_=sall[rows, :, :].bitcast(I32),
+                    )
+
+
+            with tc.tile_pool(name="io", bufs=2) as io, tc.tile_pool(name="work", bufs=2) as work, tc.tile_pool(
+                name="mxop", bufs=1
+            ) as mxop, tc.psum_pool(name="pst", bufs=1) as pst, tc.psum_pool(name="psm", bufs=1) as psm:
+                for c in range(NCH):
+                    xraw = io.tile([P, CH_ROWS, I], BF16, tag="xraw", bufs=2)
+                    nc.sync.dma_start(out=xraw[:], in_=xv[:, c * CH_ROWS : (c + 1) * CH_ROWS, :])
+                    xw = (
+                        xraw[:]
+                        .rearrange("p r i -> p (r i)")
+                        .bitcast(F32)
+                        .rearrange("p (s m u) -> p s m u", s=SUP, m=P, u=2)
+                    )
+                    xp = io.tile([P, 4, W], BF16, tag="xp", bufs=2)
+                    for u in range(2):
+                        psx = pst.tile([P, W], F32, tag="psx", bufs=2)
+                        for s in range(SUP):
+                            nc.tensor.transpose(psx[:, s * P : (s + 1) * P], xw[:, s, :, u], ident_f[:])
+                        nc.scalar.copy(
+                            out=xp[:, 2 * u : 2 * u + 2, :],
+                            in_=psx[:].bitcast(BF16).rearrange("p (c e) -> p e c", e=2),
+                        )
+                    xT = io.tile([P, CH_ROWS * P], BF16, tag="xT", bufs=2)
+                    for half in range(CH_ROWS // 8):
+                        psb = pst.tile([P, 8 * P], BF16, tag="psb", bufs=1)
+                        for rr in range(8):
+                            nc.tensor.transpose(psb[:, rr * P : (rr + 1) * P], xraw[:, half * 8 + rr, :], ident_b[:])
+                        nc.scalar.copy(out=xT[:, half * 8 * P : (half + 1) * 8 * P], in_=psb[:])
+
+                    cub = {}
+                    left = {}
+                    vee = {}
+                    codes = {}
+                    scales = {}
+                    for j in range(NKN):
+                        for t in range(4):
+                            sq = work.tile([P, W], F32, tag="sq", bufs=3)
+                            nc.scalar.activation(out=sq[:], in_=xp[:, t, :], func=AF.Square, bias=nk[:, t, j : j + 1], scale=1.0)
+                            cj = work.tile([P, W], F32, name="cj", tag="c%d" % t, bufs=3)
+                            nc.vector.scalar_tensor_tensor(
+                                out=cj[:], in0=xp[:, t, :], scalar=kn[:, t, j : j + 1], in1=sq[:], op0=ALU.subtract, op1=ALU.mult
+                            )
+                            cub[(j, t)] = cj
+                        if 1 <= j <= 8:
+                            k = j - 1
+                            for t in range(4):
+                                uu = work.tile([P, W], F32, tag="uu", bufs=3)
+                                nc.scalar.activation(out=uu[:], in_=cub[(j, t)][:], func=AF.Relu, scale=a1[:, t, k : k + 1])
+                                lf = work.tile([P, W], BF16, name="lf", tag="l%d" % t, bufs=5)
+                                nc.vector.scalar_tensor_tensor(
+                                    out=lf[:], in0=cub[(j - 1, t)][:], scalar=a0[:, t, k : k + 1], in1=uu[:], op0=ALU.mult, op1=ALU.subtract
+                                )
+                                left[(k, t)] = lf
+                        if j >= 4:
+                            k = j - 4
+                            npl = work.tile([P, 4, W], BF16, tag="npl", bufs=2)
+                            for t in range(4):
+                                rt = work.tile([P, W], BF16, tag="rt", bufs=3)
+                                nc.vector.scalar_tensor_tensor(
+                                    out=rt[:], in0=cub[(j, t)][:], scalar=nb4[:, t, k : k + 1], in1=vee[(k, t)][:], op0=ALU.mult, op1=ALU.subtract
+                                )
+                                nc.vector.tensor_tensor(out=npl[:, t, :], in0=left[(k, t)][:], in1=rt[:], op=ALU.max)
+                            grp = work.tile([P, 4 * W], BF16, tag="grp", bufs=2, align_bytes=64)
+                            gdst = grp[:].rearrange("p (c i t) -> p c t i", i=4, t=4)
+                            gsrc2 = npl[:].rearrange("p t (c i) -> p c t i", i=4)
+                            if k in ACT_REGROUP:
+                                nc.scalar.activation(out=gdst, in_=gsrc2, func=AF.Relu)
+                            else:
+                                nc.vector.tensor_scalar(out=gdst, in0=gsrc2, scalar1=0.0, scalar2=None, op0=ALU.max)
+                            cd = mxop.tile([P, W], U32, name="cd", tag="cd%d" % k, bufs=1, align_bytes=64)
+                            sc = mxop.tile([P, W], U8, name="sc", tag="sc%d" % k, bufs=1, align_bytes=64)
+                            nc.vector.quantize_mx(out=cd[:].bitcast(FP8X4), scales=sc[:], in_=grp[:])
+                            codes[k] = cd
+                            scales[k] = sc
+                        if 3 <= j <= 10:
+                            k = j - 3
+                            for t in range(4):
+                                vv = work.tile([P, W], F32, name="vv", tag="v%d" % t, bufs=2)
+                                nc.scalar.activation(out=vv[:], in_=cub[(j, t)][:], func=AF.Relu, scale=nb3[:, t, k : k + 1])
+                                vee[(k, t)] = vv
+
+                    if c == 0:
+                        prepare_coef()
+                    for s in range(SUP):
+                        osb = io.tile([P, 4, O], F32, tag="osb", bufs=2)
+                        osf = osb[:].rearrange("p r o -> p (r o)")
+                        for q in range(2):
+                            psbase = psm.tile([P, 2 * O], F32, tag="psbase", bufs=2)
+                            for h in range(2):
+                                row = 4 * s + 2 * q + h
+                                nc.tensor.matmul(
+                                    out=psbase[:, h * O : (h + 1) * O],
+                                    lhsT=xT[:, row * P : (row + 1) * P],
+                                    rhs=bw[:],
+                                    start=True,
+                                    stop=True,
+                                )
+                            acc = psm.tile([P, 2 * O], F32, tag="acc", bufs=3)
+                            for k in range(NC):
+                                nc.tensor.matmul_mx(
+                                    out=acc[:],
+                                    lhsT=codes[k][:, s * P : (s + 1) * P].bitcast(FP8X4),
+                                    lhsT_scale=scales[k][:, s * P : (s + 1) * P],
+                                    rhs=rh[:, k, q, :].bitcast(FP8X4),
+                                    rhs_scale=rhs_sc[:, k, q, :],
+                                    start=(k == 0),
+                                    stop=(k == NC - 1),
+                                )
+                            tmp = work.tile([P, 2 * O], F32, tag="tmp", bufs=2)
+                            nc.vector.tensor_tensor(
+                                out=tmp[:], in0=psbase[:], in1=bias2[:].rearrange("p h o -> p (h o)"), op=ALU.add
+                            )
+                            nc.vector.tensor_tensor(
+                                out=osf[:, q * 2 * O : (q + 1) * 2 * O], in0=acc[:], in1=tmp[:], op=ALU.add
+                            )
+                        r0 = c * CH_ROWS + 4 * s
+                        nc.sync.dma_start(out=ov[:, r0 : r0 + 4, :], in_=osb[:])

@@ -19,7 +19,7 @@ CH_ROWS = 4 * SUP
 NCH = ROWS // CH_ROWS
 W = SUP * P
 NKN = 12
-ACT_REGROUP = (0, 1, 2, 3, 4, 5, 6)
+ACT_REGROUP = (0, 2, 4, 6)
 
 
 def tile_kanlinear_t_kernel(tc, x, grid, coef, base_weight, base_bias, out):

@@ -19,7 +19,7 @@ CH_ROWS = 4 * SUP
 NCH = ROWS // CH_ROWS
 W = SUP * P
 NKN = 12
-ACT_REGROUP = (0, 2, 4, 6)
+ACT_REGROUP = (0, 1, 2, 3, 4, 5, 6)
 
 
 def tile_kanlinear_t_kernel(tc, x, grid, coef, base_weight, base_bias, out):
@@ -141,15 +141,16 @@ def tile_kanlinear_t_kernel(tc, x, grid, coef, base_weight, base_bias, out):
                         .bitcast(F32)
                         .rearrange("p (s m u) -> p s m u", s=SUP, m=P, u=2)
                     )
-                    xp = io.tile([P, 4, W], BF16, tag="xp", bufs=2)
+                    xa = []
+                    xd = []
                     for u in range(2):
-                        psx = pst.tile([P, W], F32, tag="psx", bufs=2)
-                        for s in range(SUP):
-                            nc.tensor.transpose(psx[:, s * P : (s + 1) * P], xw[:, s, :, u], ident_f[:])
-                        nc.scalar.copy(
-                            out=xp[:, 2 * u : 2 * u + 2, :],
-                            in_=psx[:].bitcast(BF16).rearrange("p (c e) -> p e c", e=2),
-                        )
+                        for planes, tg in ((xa, "psxa%d" % u), (xd, "psxd%d" % u)):
+                            psx = pst.tile([P, W], F32, name="psx", tag=tg, bufs=1)
+                            for s in range(SUP):
+                                nc.tensor.transpose(psx[:, s * P : (s + 1) * P], xw[:, s, :, u], ident_f[:])
+                            pv = psx[:].bitcast(BF16).rearrange("p (c e) -> p e c", e=2)
+                            planes.append(pv[:, 0, :])
+                            planes.append(pv[:, 1, :])
                     xT = io.tile([P, CH_ROWS * P], BF16, tag="xT", bufs=2)
                     for half in range(CH_ROWS // 8):
                         psb = pst.tile([P, 8 * P], BF16, tag="psb", bufs=1)
@@ -165,10 +166,10 @@ def tile_kanlinear_t_kernel(tc, x, grid, coef, base_weight, base_bias, out):
                     for j in range(NKN):
                         for t in range(4):
                             sq = work.tile([P, W], F32, tag="sq", bufs=3)
-                            nc.scalar.activation(out=sq[:], in_=xp[:, t, :], func=AF.Square, bias=nk[:, t, j : j + 1], scale=1.0)
+                            nc.scalar.activation(out=sq[:], in_=xa[t], func=AF.Square, bias=nk[:, t, j : j + 1], scale=1.0)
                             cj = work.tile([P, W], F32, name="cj", tag="c%d" % t, bufs=3)
                             nc.vector.scalar_tensor_tensor(
-                                out=cj[:], in0=xp[:, t, :], scalar=kn[:, t, j : j + 1], in1=sq[:], op0=ALU.subtract, op1=ALU.mult
+                                out=cj[:], in0=xd[t], scalar=kn[:, t, j : j + 1], in1=sq[:], op0=ALU.subtract, op1=ALU.mult
                             )
                             cub[(j, t)] = cj
                         if 1 <= j <= 8:
@@ -215,7 +216,7 @@ def tile_kanlinear_t_kernel(tc, x, grid, coef, base_weight, base_bias, out):
                         osb = io.tile([P, 4, O], F32, tag="osb", bufs=2)
                         osf = osb[:].rearrange("p r o -> p (r o)")
                         for q in range(2):
-                            psbase = psm.tile([P, 2 * O], F32, tag="psbase", bufs=2)
+                            psbase = psm.tile([P, 2 * O], F32, tag="psbase", bufs=1)
                             for h in range(2):
                                 row = 4 * s + 2 * q + h
                                 nc.tensor.matmul(
@@ -225,7 +226,7 @@ def tile_kanlinear_t_kernel(tc, x, grid, coef, base_weight, base_bias, out):
                                     start=True,
                                     stop=True,
                                 )
-                            acc = psm.tile([P, 2 * O], F32, tag="acc", bufs=3)
+                            acc = psm.tile([P, 2 * O], F32, tag="acc", bufs=2)
                             for k in range(NC):
                                 nc.tensor.matmul_mx(
                                     out=acc[:],

@@ -19,7 +19,6 @@ CH_ROWS = 4 * SUP
 NCH = ROWS // CH_ROWS
 W = SUP * P
 NKN = 12
-ACT_REGROUP = (0, 1, 2, 3, 4, 5, 6)
 
 
 def tile_kanlinear_t_kernel(tc, x, grid, coef, base_weight, base_bias, out):
@@ -194,10 +193,7 @@ def tile_kanlinear_t_kernel(tc, x, grid, coef, base_weight, base_bias, out):
                             grp = work.tile([P, 4 * W], BF16, tag="grp", bufs=2, align_bytes=64)
                             gdst = grp[:].rearrange("p (c i t) -> p c t i", i=4, t=4)
                             gsrc2 = npl[:].rearrange("p t (c i) -> p c t i", i=4)
-                            if k in ACT_REGROUP:
-                                nc.scalar.activation(out=gdst, in_=gsrc2, func=AF.Relu)
-                            else:
-                                nc.vector.tensor_scalar(out=gdst, in0=gsrc2, scalar1=0.0, scalar2=None, op0=ALU.max)
+                            nc.gpsimd.tensor_scalar(out=gdst, in0=gsrc2, scalar1=3.0e38, scalar2=0.0, op0=ALU.min, op1=ALU.max)
                             cd = mxop.tile([P, W], U32, name="cd", tag="cd%d" % k, bufs=1, align_bytes=64)
                             sc = mxop.tile([P, W], U8, name="sc", tag="sc%d" % k, bufs=1, align_bytes=64)
                             nc.vector.quantize_mx(out=cd[:].bitcast(FP8X4), scales=sc[:], in_=grp[:])

@@ -19,6 +19,7 @@ CH_ROWS = 4 * SUP
 NCH = ROWS // CH_ROWS
 W = SUP * P
 NKN = 12
+ACT_REGROUP = (0, 1, 2, 3, 4, 5, 6)
 
 
 def tile_kanlinear_t_kernel(tc, x, grid, coef, base_weight, base_bias, out):
@@ -130,8 +131,22 @@ def tile_kanlinear_t_kernel(tc, x, grid, coef, base_weight, base_bias, out):
 
             with tc.tile_pool(name="io", bufs=2) as io, tc.tile_pool(name="work", bufs=2) as work, tc.tile_pool(
                 name="mxop", bufs=1
-            ) as mxop, tc.psum_pool(name="pst", bufs=1) as pst, tc.psum_pool(name="psm", bufs=1) as psm:
+            ) as mxop, tc.psum_pool(name="ps", bufs=8) as ps:
+                bias_row = bias2[:].rearrange("p h o -> p (h o)")
+
+                def mx_pass(acc, cd, sc, s, q, k):
+                    nc.tensor.matmul_mx(
+                        out=acc[:],
+                        lhsT=cd[:, s * P : (s + 1) * P].bitcast(FP8X4),
+                        lhsT_scale=sc[:, s * P : (s + 1) * P],
+                        rhs=rh[:, k, q, :].bitcast(FP8X4),
+                        rhs_scale=rhs_sc[:, k, q, :],
+                        start=(k == 0),
+                        stop=(k == NC - 1),
+                    )
+
                 for c in range(NCH):
+                    last = c == NCH - 1
                     xraw = io.tile([P, CH_ROWS, I], BF16, tag="xraw", bufs=2)
                     nc.sync.dma_start(out=xraw[:], in_=xv[:, c * CH_ROWS : (c + 1) * CH_ROWS, :])
                     xw = (
@@ -140,65 +155,107 @@ def tile_kanlinear_t_kernel(tc, x, grid, coef, base_weight, base_bias, out):
                         .bitcast(F32)
                         .rearrange("p (s m u) -> p s m u", s=SUP, m=P, u=2)
                     )
-                    xa = []
-                    xd = []
+                    xp = io.tile([P, 4, W], BF16, tag="xp", bufs=2)
                     for u in range(2):
-                        for planes, tg in ((xa, "psxa%d" % u), (xd, "psxd%d" % u)):
-                            psx = pst.tile([P, W], F32, name="psx", tag=tg, bufs=1)
-                            for s in range(SUP):
-                                nc.tensor.transpose(psx[:, s * P : (s + 1) * P], xw[:, s, :, u], ident_f[:])
-                            pv = psx[:].bitcast(BF16).rearrange("p (c e) -> p e c", e=2)
-                            planes.append(pv[:, 0, :])
-                            planes.append(pv[:, 1, :])
+                        psx = ps.tile([P, W], F32, name="psx", tag="bank")
+                        for s in range(SUP):
+                            nc.tensor.transpose(psx[:, s * P : (s + 1) * P], xw[:, s, :, u], ident_f[:])
+                        nc.scalar.copy(
+                            out=xp[:, 2 * u : 2 * u + 2, :],
+                            in_=psx[:].bitcast(BF16).rearrange("p (c e) -> p e c", e=2),
+                        )
                     xT = io.tile([P, CH_ROWS * P], BF16, tag="xT", bufs=2)
                     for half in range(CH_ROWS // 8):
-                        psb = pst.tile([P, 8 * P], BF16, tag="psb", bufs=1)
+                        psb = ps.tile([P, 8 * P], BF16, name="psb", tag="bank")
                         for rr in range(8):
                             nc.tensor.transpose(psb[:, rr * P : (rr + 1) * P], xraw[:, half * 8 + rr, :], ident_b[:])
                         nc.scalar.copy(out=xT[:, half * 8 * P : (half + 1) * 8 * P], in_=psb[:])
 
+                    outs = []
+
+                    def base_part(s):
+                        osb = io.tile([P, 4 * O], F32, name="osb", tag="osb", bufs=4)
+                        outs.append(osb)
+                        for q in range(2):
+                            psbase = ps.tile([P, 2 * O], F32, name="psbase", tag="bank")
+                            for h in range(2):
+                                row = 4 * s + 2 * q + h
+                                nc.tensor.matmul(
+                                    out=psbase[:, h * O : (h + 1) * O],
+                                    lhsT=xT[:, row * P : (row + 1) * P],
+                                    rhs=bw[:],
+                                    start=True,
+                                    stop=True,
+                                )
+                            nc.vector.tensor_tensor(
+                                out=osb[:, q * 2 * O : (q + 1) * 2 * O], in0=psbase[:], in1=bias_row, op=ALU.add
+                            )
+
+                    def close(s, q, acc):
+                        part = outs[s][:, q * 2 * O : (q + 1) * 2 * O]
+                        nc.vector.tensor_tensor(out=part, in0=acc[:], in1=part, op=ALU.add)
+                        if q == 1:
+                            r0 = c * CH_ROWS + 4 * s
+                            nc.sync.dma_start(
+                                out=ov[:, r0 : r0 + 4, :], in_=outs[s][:].rearrange("p (r o) -> p r o", o=O)
+                            )
+
+                    accs = []
+                    if last:
+                        for s in range(SUP):
+                            base_part(s)
+
                     cub = {}
-                    left = {}
+                    planes = {}
                     vee = {}
                     codes = {}
                     scales = {}
                     for j in range(NKN):
                         for t in range(4):
-                            sq = work.tile([P, W], F32, tag="sq", bufs=3)
-                            nc.scalar.activation(out=sq[:], in_=xa[t], func=AF.Square, bias=nk[:, t, j : j + 1], scale=1.0)
+                            sq = work.tile([P, W], F32, tag="sq", bufs=4)
+                            nc.scalar.activation(out=sq[:], in_=xp[:, t, :], func=AF.Square, bias=nk[:, t, j : j + 1], scale=1.0)
                             cj = work.tile([P, W], F32, name="cj", tag="c%d" % t, bufs=3)
                             nc.vector.scalar_tensor_tensor(
-                                out=cj[:], in0=xd[t], scalar=kn[:, t, j : j + 1], in1=sq[:], op0=ALU.subtract, op1=ALU.mult
+                                out=cj[:], in0=xp[:, t, :], scalar=kn[:, t, j : j + 1], in1=sq[:], op0=ALU.subtract, op1=ALU.mult
                             )
                             cub[(j, t)] = cj
                         if 1 <= j <= 8:
                             k = j - 1
+                            npl = work.tile([P, 4, W], BF16, tag="npl", bufs=5)
+                            planes[k] = npl
                             for t in range(4):
-                                uu = work.tile([P, W], F32, tag="uu", bufs=3)
+                                uu = work.tile([P, W], F32, tag="uu", bufs=4)
                                 nc.scalar.activation(out=uu[:], in_=cub[(j, t)][:], func=AF.Relu, scale=a1[:, t, k : k + 1])
-                                lf = work.tile([P, W], BF16, name="lf", tag="l%d" % t, bufs=5)
                                 nc.vector.scalar_tensor_tensor(
-                                    out=lf[:], in0=cub[(j - 1, t)][:], scalar=a0[:, t, k : k + 1], in1=uu[:], op0=ALU.mult, op1=ALU.subtract
+                                    out=npl[:, t, :], in0=cub[(j - 1, t)][:], scalar=a0[:, t, k : k + 1], in1=uu[:], op0=ALU.mult, op1=ALU.subtract
                                 )
-                                left[(k, t)] = lf
                         if j >= 4:
                             k = j - 4
-                            npl = work.tile([P, 4, W], BF16, tag="npl", bufs=2)
+                            npl = planes[k]
+                            rt = work.tile([P, 4, W], BF16, tag="rt", bufs=2)
                             for t in range(4):
-                                rt = work.tile([P, W], BF16, tag="rt", bufs=3)
                                 nc.vector.scalar_tensor_tensor(
-                                    out=rt[:], in0=cub[(j, t)][:], scalar=nb4[:, t, k : k + 1], in1=vee[(k, t)][:], op0=ALU.mult, op1=ALU.subtract
+                                    out=rt[:, t, :], in0=cub[(j, t)][:], scalar=nb4[:, t, k : k + 1], in1=vee[(k, t)][:], op0=ALU.mult, op1=ALU.subtract
                                 )
-                                nc.vector.tensor_tensor(out=npl[:, t, :], in0=left[(k, t)][:], in1=rt[:], op=ALU.max)
+                            nc.vector.tensor_tensor(out=npl[:], in0=npl[:], in1=rt[:], op=ALU.max)
                             grp = work.tile([P, 4 * W], BF16, tag="grp", bufs=2, align_bytes=64)
                             gdst = grp[:].rearrange("p (c i t) -> p c t i", i=4, t=4)
                             gsrc2 = npl[:].rearrange("p t (c i) -> p c t i", i=4)
-                            nc.gpsimd.tensor_scalar(out=gdst, in0=gsrc2, scalar1=3.0e38, scalar2=0.0, op0=ALU.min, op1=ALU.max)
+                            if k in ACT_REGROUP:
+                                nc.scalar.activation(out=gdst, in_=gsrc2, func=AF.Relu)
+                            else:
+                                nc.vector.tensor_scalar(out=gdst, in0=gsrc2, scalar1=0.0, scalar2=None, op0=ALU.max)
                             cd = mxop.tile([P, W], U32, name="cd", tag="cd%d" % k, bufs=1, align_bytes=64)
                             sc = mxop.tile([P, W], U8, name="sc", tag="sc%d" % k, bufs=1, align_bytes=64)
                             nc.vector.quantize_mx(out=cd[:].bitcast(FP8X4), scales=sc[:], in_=grp[:])
                             codes[k] = cd
                             scales[k] = sc
+                            if last:
+                                for g in range(2 * SUP):
+                                    if k == 0:
+                                        acc = ps.tile([P, 2 * O], F32, name="acc", tag="bank")
+                                        accs.append(acc)
+                                    mx_pass(accs[g], cd, sc, g // 2, g % 2, k)
                         if 3 <= j <= 10:
                             k = j - 3
                             for t in range(4):
@@ -209,36 +266,13 @@ def tile_kanlinear_t_kernel(tc, x, grid, coef, base_weight, base_bias, out):
                     if c == 0:
                         prepare_coef()
                     for s in range(SUP):
-                        osb = io.tile([P, 4, O], F32, tag="osb", bufs=2)
-                        osf = osb[:].rearrange("p r o -> p (r o)")
+                        if not last:
+                            base_part(s)
                         for q in range(2):
-                            psbase = psm.tile([P, 2 * O], F32, tag="psbase", bufs=1)
-                            for h in range(2):
-                                row = 4 * s + 2 * q + h
-                                nc.tensor.matmul(
-                                    out=psbase[:, h * O : (h + 1) * O],
-                                    lhsT=xT[:, row * P : (row + 1) * P],
-                                    rhs=bw[:],
-                                    start=True,
-                                    stop=True,
-                                )
-                            acc = psm.tile([P, 2 * O], F32, tag="acc", bufs=2)
-                            for k in range(NC):
-                                nc.tensor.matmul_mx(
-                                    out=acc[:],
-                                    lhsT=codes[k][:, s * P : (s + 1) * P].bitcast(FP8X4),
-                                    lhsT_scale=scales[k][:, s * P : (s + 1) * P],
-                                    rhs=rh[:, k, q, :].bitcast(FP8X4),
-                                    rhs_scale=rhs_sc[:, k, q, :],
-                                    start=(k == 0),
-                                    stop=(k == NC - 1),
-                                )
-                            tmp = work.tile([P, 2 * O], F32, tag="tmp", bufs=2)
-                            nc.vector.tensor_tensor(
-                                out=tmp[:], in0=psbase[:], in1=bias2[:].rearrange("p h o -> p (h o)"), op=ALU.add
-                            )
-                            nc.vector.tensor_tensor(
-                                out=osf[:, q * 2 * O : (q + 1) * 2 * O], in0=acc[:], in1=tmp[:], op=ALU.add
-                            )
-                        r0 = c * CH_ROWS + 4 * s
-                        nc.sync.dma_start(out=ov[:, r0 : r0 + 4, :], in_=osb[:])
+                            if last:
+                                acc = accs[2 * s + q]
+                            else:
+                                acc = ps.tile([P, 2 * O], F32, name="acc", tag="bank")
+                                for k in range(NC):
+                                    mx_pass(acc, codes[k], scales[k], s, q, k)
+                            close(s, q, acc)

@@ -19,7 +19,8 @@ CH_ROWS = 4 * SUP
 NCH = ROWS // CH_ROWS
 W = SUP * P
 NKN = 12
-ACT_REGROUP = (0, 1, 2, 3, 4, 5, 6)
+LAST_TAGS = (("bank", 5),) * 5 + (("psx", 2),) * 2 + (("psb", 1),)
+ACT_REGROUP = (0, 1, 2, 4, 5, 6)
 
 
 def tile_kanlinear_t_kernel(tc, x, grid, coef, base_weight, base_bias, out):
@@ -131,8 +132,15 @@ def tile_kanlinear_t_kernel(tc, x, grid, coef, base_weight, base_bias, out):
 
             with tc.tile_pool(name="io", bufs=2) as io, tc.tile_pool(name="work", bufs=2) as work, tc.tile_pool(
                 name="mxop", bufs=1
-            ) as mxop, tc.psum_pool(name="ps", bufs=8) as ps:
-                bias_row = bias2[:].rearrange("p h o -> p (h o)")
+            ) as mxop, tc.psum_pool(name="ps", bufs=1) as ps:
+                bias_t = const.tile([P, 2, P], F32)
+
+                def prepare_bias():
+                    for h in range(2):
+                        pbt = ps.tile([P, P], F32, name="pbt", tag="psx", bufs=2)
+                        nc.tensor.transpose(pbt[:], bias2[:, 0, h * P : (h + 1) * P], ident_f[:])
+                        nc.vector.tensor_copy(out=bias_t[:, h, :], in_=pbt[:])
+
 
                 def mx_pass(acc, cd, sc, s, q, k):
                     nc.tensor.matmul_mx(
@@ -157,7 +165,7 @@ def tile_kanlinear_t_kernel(tc, x, grid, coef, base_weight, base_bias, out):
                     )
                     xp = io.tile([P, 4, W], BF16, tag="xp", bufs=2)
                     for u in range(2):
-                        psx = ps.tile([P, W], F32, name="psx", tag="bank")
+                        psx = ps.tile([P, W], F32, name="psx", tag="psx", bufs=2)
                         for s in range(SUP):
                             nc.tensor.transpose(psx[:, s * P : (s + 1) * P], xw[:, s, :, u], ident_f[:])
                         nc.scalar.copy(
@@ -166,7 +174,7 @@ def tile_kanlinear_t_kernel(tc, x, grid, coef, base_weight, base_bias, out):
                         )
                     xT = io.tile([P, CH_ROWS * P], BF16, tag="xT", bufs=2)
                     for half in range(CH_ROWS // 8):
-                        psb = ps.tile([P, 8 * P], BF16, name="psb", tag="bank")
+                        psb = ps.tile([P, 8 * P], BF16, name="psb", tag="psb", bufs=1)
                         for rr in range(8):
                             nc.tensor.transpose(psb[:, rr * P : (rr + 1) * P], xraw[:, half * 8 + rr, :], ident_b[:])
                         nc.scalar.copy(out=xT[:, half * 8 * P : (half + 1) * 8 * P], in_=psb[:])
@@ -177,19 +185,26 @@ def tile_kanlinear_t_kernel(tc, x, grid, coef, base_weight, base_bias, out):
                         osb = io.tile([P, 4 * O], F32, name="osb", tag="osb", bufs=4)
                         outs.append(osb)
                         for q in range(2):
-                            psbase = ps.tile([P, 2 * O], F32, name="psbase", tag="bank")
+                            psbase = ps.tile([P, 2 * O], F32, name="psbase", tag="bank", bufs=5)
+                            for w in range(4):
+                                nc.tensor.matmul(
+                                    out=psbase[:, w * P : (w + 1) * P],
+                                    lhsT=bias_t[:, w % 2, :],
+                                    rhs=ident_f[:],
+                                    is_transpose=True,
+                                    start=(w == 0),
+                                    stop=False,
+                                )
                             for h in range(2):
                                 row = 4 * s + 2 * q + h
                                 nc.tensor.matmul(
                                     out=psbase[:, h * O : (h + 1) * O],
                                     lhsT=xT[:, row * P : (row + 1) * P],
                                     rhs=bw[:],
-                                    start=True,
-                                    stop=True,
+                                    start=False,
+                                    stop=(h == 1),
                                 )
-                            nc.vector.tensor_tensor(
-                                out=osb[:, q * 2 * O : (q + 1) * 2 * O], in0=psbase[:], in1=bias_row, op=ALU.add
-                            )
+                            nc.scalar.copy(out=osb[:, q * 2 * O : (q + 1) * 2 * O], in_=psbase[:])
 
                     def close(s, q, acc):
                         part = outs[s][:, q * 2 * O : (q + 1) * 2 * O]
@@ -253,7 +268,7 @@ def tile_kanlinear_t_kernel(tc, x, grid, coef, base_weight, base_bias, out):
                             if last:
                                 for g in range(2 * SUP):
                                     if k == 0:
-                                        acc = ps.tile([P, 2 * O], F32, name="acc", tag="bank")
+                                        acc = ps.tile([P, 2 * O], F32, name="acc", tag=LAST_TAGS[g][0], bufs=LAST_TAGS[g][1])
                                         accs.append(acc)
                                     mx_pass(accs[g], cd, sc, g // 2, g % 2, k)
                         if 3 <= j <= 10:
@@ -264,6 +279,7 @@ def tile_kanlinear_t_kernel(tc, x, grid, coef, base_weight, base_bias, out):
                                 vee[(k, t)] = vv
 
                     if c == 0:
+                        prepare_bias()
                         prepare_coef()
                     for s in range(SUP):
                         if not last:
@@ -272,7 +288,7 @@ def tile_kanlinear_t_kernel(tc, x, grid, coef, base_weight, base_bias, out):
                             if last:
                                 acc = accs[2 * s + q]
                             else:
-                                acc = ps.tile([P, 2 * O], F32, name="acc", tag="bank")
+                                acc = ps.tile([P, 2 * O], F32, name="acc", tag="bank", bufs=5)
                                 for k in range(NC):
                                     mx_pass(acc, codes[k], scales[k], s, q, k)
                             close(s, q, acc)

@@ -42,6 +42,8 @@ def tile_kanlinear_t_kernel(tc, x, grid, coef, base_weight, base_bias, out):
         bias2 = const.tile([P, 2, O], F32)
         rh = const.tile([P, NC, 2, 2 * O], U32, align_bytes=64)
         rhs_sc = const.tile([P, NC, 2, 2 * O], U8, align_bytes=64)
+        nc.vector.memset(rh[:].rearrange("p k q w -> p (k q w)").bitcast(I32), 0)
+        nc.vector.memset(rhs_sc[:].rearrange("p k q w -> p (k q w)").bitcast(I32), 0)
 
         with tc.tile_pool(name="prep", bufs=1) as prep:
             g_bf = prep.tile([P, 24], BF16)
@@ -104,8 +106,6 @@ def tile_kanlinear_t_kernel(tc, x, grid, coef, base_weight, base_bias, out):
                 nc.vector.tensor_copy(out=bias2[:, h, :], in_=bias_bf[:])
 
             def prepare_coef():
-                nc.vector.memset(rh[:].rearrange("p k q w -> p (k q w)").bitcast(I32), 0)
-                nc.vector.memset(rhs_sc[:].rearrange("p k q w -> p (k q w)").bitcast(I32), 0)
                 cv = craw[:].rearrange("p (t o k) -> p t o k", t=4, o=O, k=NC)
                 call = prep.tile([P, NC, O], U32, align_bytes=64)
                 sall = prep.tile([P, NC, O], U8, align_bytes=64)
@@ -222,12 +222,11 @@ def tile_kanlinear_t_kernel(tc, x, grid, coef, base_weight, base_bias, out):
 
                     cub = {}
                     planes = {}
-                    vee = {}
                     codes = {}
                     scales = {}
                     for j in range(NKN):
                         for t in range(4):
-                            sq = work.tile([P, W], F32, tag="sq", bufs=4)
+                            sq = work.tile([P, W], F32, tag="sq", bufs=6)
                             nc.scalar.activation(out=sq[:], in_=xp[:, t, :], func=AF.Square, bias=nk[:, t, j : j + 1], scale=1.0)
                             cj = work.tile([P, W], F32, name="cj", tag="c%d" % t, bufs=3)
                             nc.vector.scalar_tensor_tensor(
@@ -239,7 +238,7 @@ def tile_kanlinear_t_kernel(tc, x, grid, coef, base_weight, base_bias, out):
                             npl = work.tile([P, 4, W], BF16, tag="npl", bufs=5)
                             planes[k] = npl
                             for t in range(4):
-                                uu = work.tile([P, W], F32, tag="uu", bufs=4)
+                                uu = work.tile([P, W], F32, tag="uu", bufs=8)
                                 nc.scalar.activation(out=uu[:], in_=cub[(j, t)][:], func=AF.Relu, scale=a1[:, t, k : k + 1])
                                 nc.vector.scalar_tensor_tensor(
                                     out=npl[:, t, :], in0=cub[(j - 1, t)][:], scalar=a0[:, t, k : k + 1], in1=uu[:], op0=ALU.mult, op1=ALU.subtract
@@ -249,8 +248,10 @@ def tile_kanlinear_t_kernel(tc, x, grid, coef, base_weight, base_bias, out):
                             npl = planes[k]
                             rt = work.tile([P, 4, W], BF16, tag="rt", bufs=2)
                             for t in range(4):
+                                vv = work.tile([P, W], F32, name="vv", tag="uu", bufs=8)
+                                nc.scalar.activation(out=vv[:], in_=cub[(j - 1, t)][:], func=AF.Relu, scale=nb3[:, t, k : k + 1])
                                 nc.vector.scalar_tensor_tensor(
-                                    out=rt[:, t, :], in0=cub[(j, t)][:], scalar=nb4[:, t, k : k + 1], in1=vee[(k, t)][:], op0=ALU.mult, op1=ALU.subtract
+                                    out=rt[:, t, :], in0=cub[(j, t)][:], scalar=nb4[:, t, k : k + 1], in1=vv[:], op0=ALU.mult, op1=ALU.subtract
                                 )
                             nc.vector.tensor_tensor(out=npl[:], in0=npl[:], in1=rt[:], op=ALU.max)
                             grp = work.tile([P, 4 * W], BF16, tag="grp", bufs=2, align_bytes=64)
@@ -271,12 +272,6 @@ def tile_kanlinear_t_kernel(tc, x, grid, coef, base_weight, base_bias, out):
                                         acc = ps.tile([P, 2 * O], F32, name="acc", tag=LAST_TAGS[g][0], bufs=LAST_TAGS[g][1])
                                         accs.append(acc)
                                     mx_pass(accs[g], cd, sc, g // 2, g % 2, k)
-                        if 3 <= j <= 10:
-                            k = j - 3
-                            for t in range(4):
-                                vv = work.tile([P, W], F32, name="vv", tag="v%d" % t, bufs=2)
-                                nc.scalar.activation(out=vv[:], in_=cub[(j, t)][:], func=AF.Relu, scale=nb3[:, t, k : k + 1])
-                                vee[(k, t)] = vv
 
                     if c == 0:
                         prepare_bias()

@@ -20,7 +20,7 @@ NCH = ROWS // CH_ROWS
 W = SUP * P
 NKN = 12
 LAST_TAGS = (("bank", 5),) * 5 + (("psx", 2),) * 2 + (("psb", 1),)
-ACT_REGROUP = (0, 1, 2, 4, 5, 6)
+ACT_REGROUP = (0, 1, 3, 4, 6)
 
 
 def tile_kanlinear_t_kernel(tc, x, grid, coef, base_weight, base_bias, out):

@@ -153,8 +153,104 @@ def tile_kanlinear_t_kernel(tc, x, grid, coef, base_weight, base_bias, out):
                         stop=(k == NC - 1),
                     )
 
+                pending = []
+                issued = [0]
+
+                def gap():
+                    if issued[0] < len(pending):
+                        op = pending[issued[0]]
+                        issued[0] += 1
+                        op()
+
+                def base_part(st, s):
+                    osb = io.tile([P, 4 * O], F32, name="osb", tag="osb", bufs=4)
+                    st["outs"].append(osb)
+                    xT = st["xT"]
+                    for q in range(2):
+                        psbase = ps.tile([P, 2 * O], F32, name="psbase", tag="bank", bufs=5)
+                        for w in range(4):
+                            nc.tensor.matmul(
+                                out=psbase[:, w * P : (w + 1) * P],
+                                lhsT=bias_t[:, w % 2, :],
+                                rhs=ident_f[:],
+                                is_transpose=True,
+                                start=(w == 0),
+                                stop=False,
+                            )
+                        for h in range(2):
+                            row = 4 * s + 2 * q + h
+                            nc.tensor.matmul(
+                                out=psbase[:, h * O : (h + 1) * O],
+                                lhsT=xT[:, row * P : (row + 1) * P],
+                                rhs=bw[:],
+                                start=False,
+                                stop=(h == 1),
+                            )
+                        nc.scalar.copy(out=osb[:, q * 2 * O : (q + 1) * 2 * O], in_=psbase[:])
+
+                def close(st, s, q, acc):
+                    part = st["outs"][s][:, q * 2 * O : (q + 1) * 2 * O]
+                    nc.vector.tensor_tensor(out=part, in0=acc[:], in1=part, op=ALU.add)
+                    if q == 1:
+                        r0 = st["c"] * CH_ROWS + 4 * s
+                        nc.sync.dma_start(
+                            out=ov[:, r0 : r0 + 4, :], in_=st["outs"][s][:].rearrange("p (r o) -> p r o", o=O)
+                        )
+
+                def max_op(npl, rt):
+                    return lambda: nc.vector.tensor_tensor(out=npl[:], in0=npl[:], in1=rt[:], op=ALU.max)
+
+                def regroup(st, k, npl):
+                    grp = work.tile([P, 4 * W], BF16, name="grp", tag="grp", bufs=2, align_bytes=64)
+                    st["grp"][k] = grp
+                    gdst = grp[:].rearrange("p (c i t) -> p c t i", i=4, t=4)
+                    gsrc2 = npl[:].rearrange("p t (c i) -> p c t i", i=4)
+                    if k in ACT_REGROUP:
+                        nc.scalar.activation(out=gdst, in_=gsrc2, func=AF.Relu)
+                    else:
+                        nc.vector.tensor_scalar(out=gdst, in0=gsrc2, scalar1=0.0, scalar2=None, op0=ALU.max)
+
+                def quantise(st, k):
+                    cd = mxop.tile([P, W], U32, name="cd", tag="cd%d" % k, bufs=1, align_bytes=64)
+                    sc = mxop.tile([P, W], U8, name="sc", tag="sc%d" % k, bufs=1, align_bytes=64)
+                    nc.vector.quantize_mx(out=cd[:].bitcast(FP8X4), scales=sc[:], in_=st["grp"][k][:])
+                    st["codes"][k] = cd
+                    st["scales"][k] = sc
+                    if st["last"]:
+                        for g in range(2 * SUP):
+                            if k == 0:
+                                acc = ps.tile([P, 2 * O], F32, name="acc", tag=LAST_TAGS[g][0], bufs=LAST_TAGS[g][1])
+                                st["accs"].append(acc)
+                            mx_pass(st["accs"][g], cd, sc, g // 2, g % 2, k)
+
+                def finish(st):
+                    for s in range(SUP):
+                        if not st["last"]:
+                            base_part(st, s)
+                        for q in range(2):
+                            if st["last"]:
+                                acc = st["accs"][2 * s + q]
+                            else:
+                                acc = ps.tile([P, 2 * O], F32, name="acc", tag="bank", bufs=5)
+                                for k in range(NC):
+                                    mx_pass(acc, st["codes"][k], st["scales"][k], s, q, k)
+                            close(st, s, q, acc)
+
+                def all_bases(st):
+                    def run():
+                        for s in range(SUP):
+                            base_part(st, s)
+
+                    return run
+
+                def defer(st, k, npl, rt):
+                    pending.append(max_op(npl, rt))
+                    pending.append(lambda: regroup(st, k, npl))
+                    pending.append(lambda: quantise(st, k))
+                    if k == NC - 1:
+                        pending.append(lambda: finish(st))
+
                 for c in range(NCH):
-                    last = c == NCH - 1
                     xraw = io.tile([P, CH_ROWS, I], BF16, tag="xraw", bufs=2)
                     nc.sync.dma_start(out=xraw[:], in_=xv[:, c * CH_ROWS : (c + 1) * CH_ROWS, :])
                     xw = (
@@ -179,52 +275,14 @@ def tile_kanlinear_t_kernel(tc, x, grid, coef, base_weight, base_bias, out):
                             nc.tensor.transpose(psb[:, rr * P : (rr + 1) * P], xraw[:, half * 8 + rr, :], ident_b[:])
                         nc.scalar.copy(out=xT[:, half * 8 * P : (half + 1) * 8 * P], in_=psb[:])
 
-                    outs = []
-
-                    def base_part(s):
-                        osb = io.tile([P, 4 * O], F32, name="osb", tag="osb", bufs=4)
-                        outs.append(osb)
-                        for q in range(2):
-                            psbase = ps.tile([P, 2 * O], F32, name="psbase", tag="bank", bufs=5)
-                            for w in range(4):
-                                nc.tensor.matmul(
-                                    out=psbase[:, w * P : (w + 1) * P],
-                                    lhsT=bias_t[:, w % 2, :],
-                                    rhs=ident_f[:],
-                                    is_transpose=True,
-                                    start=(w == 0),
-                                    stop=False,
-                                )
-                            for h in range(2):
-                                row = 4 * s + 2 * q + h
-                                nc.tensor.matmul(
-                                    out=psbase[:, h * O : (h + 1) * O],
-                                    lhsT=xT[:, row * P : (row + 1) * P],
-                                    rhs=bw[:],
-                                    start=False,
-                                    stop=(h == 1),
-                                )
-                            nc.scalar.copy(out=osb[:, q * 2 * O : (q + 1) * 2 * O], in_=psbase[:])
-
-                    def close(s, q, acc):
-                        part = outs[s][:, q * 2 * O : (q + 1) * 2 * O]
-                        nc.vector.tensor_tensor(out=part, in0=acc[:], in1=part, op=ALU.add)
-                        if q == 1:
-                            r0 = c * CH_ROWS + 4 * s
-                            nc.sync.dma_start(
-                                out=ov[:, r0 : r0 + 4, :], in_=outs[s][:].rearrange("p (r o) -> p r o", o=O)
-                            )
-
-                    accs = []
-                    if last:
-                        for s in range(SUP):
-                            base_part(s)
+                    st = {"c": c, "last": c == NCH - 1, "xT": xT, "outs": [], "accs": [], "codes": {}, "scales": {}, "grp": {}}
+                    if st["last"]:
+                        pending.append(all_bases(st))
 
                     cub = {}
                     planes = {}
-                    codes = {}
-                    scales = {}
                     for j in range(NKN):
+                        has_left = 1 <= j <= 8
                         for t in range(4):
                             sq = work.tile([P, W], F32, tag="sq", bufs=6)
                             nc.scalar.activation(out=sq[:], in_=xp[:, t, :], func=AF.Square, bias=nk[:, t, j : j + 1], scale=1.0)
@@ -233,9 +291,12 @@ def tile_kanlinear_t_kernel(tc, x, grid, coef, base_weight, base_bias, out):
                                 out=cj[:], in0=xp[:, t, :], scalar=kn[:, t, j : j + 1], in1=sq[:], op0=ALU.subtract, op1=ALU.mult
                             )
                             cub[(j, t)] = cj
-                        if 1 <= j <= 8:
+                            if t == 1 and not has_left:
+                                gap()
+                        gap()
+                        if has_left:
                             k = j - 1
-                            npl = work.tile([P, 4, W], BF16, tag="npl", bufs=5)
+                            npl = work.tile([P, 4, W], BF16, tag="npl", bufs=6)
                             planes[k] = npl
                             for t in range(4):
                                 uu = work.tile([P, W], F32, tag="uu", bufs=8)
@@ -243,47 +304,22 @@ def tile_kanlinear_t_kernel(tc, x, grid, coef, base_weight, base_bias, out):
                                 nc.vector.scalar_tensor_tensor(
                                     out=npl[:, t, :], in0=cub[(j - 1, t)][:], scalar=a0[:, t, k : k + 1], in1=uu[:], op0=ALU.mult, op1=ALU.subtract
                                 )
+                            gap()
                         if j >= 4:
                             k = j - 4
-                            npl = planes[k]
-                            rt = work.tile([P, 4, W], BF16, tag="rt", bufs=2)
+                            rt = work.tile([P, 4, W], BF16, tag="rt", bufs=3)
                             for t in range(4):
                                 vv = work.tile([P, W], F32, name="vv", tag="uu", bufs=8)
                                 nc.scalar.activation(out=vv[:], in_=cub[(j - 1, t)][:], func=AF.Relu, scale=nb3[:, t, k : k + 1])
                                 nc.vector.scalar_tensor_tensor(
                                     out=rt[:, t, :], in0=cub[(j, t)][:], scalar=nb4[:, t, k : k + 1], in1=vv[:], op0=ALU.mult, op1=ALU.subtract
                                 )
-                            nc.vector.tensor_tensor(out=npl[:], in0=npl[:], in1=rt[:], op=ALU.max)
-                            grp = work.tile([P, 4 * W], BF16, tag="grp", bufs=2, align_bytes=64)
-                            gdst = grp[:].rearrange("p (c i t) -> p c t i", i=4, t=4)
-                            gsrc2 = npl[:].rearrange("p t (c i) -> p c t i", i=4)
-                            if k in ACT_REGROUP:
-                                nc.scalar.activation(out=gdst, in_=gsrc2, func=AF.Relu)
-                            else:
-                                nc.vector.tensor_scalar(out=gdst, in0=gsrc2, scalar1=0.0, scalar2=None, op0=ALU.max)
-                            cd = mxop.tile([P, W], U32, name="cd", tag="cd%d" % k, bufs=1, align_bytes=64)
-                            sc = mxop.tile([P, W], U8, name="sc", tag="sc%d" % k, bufs=1, align_bytes=64)
-                            nc.vector.quantize_mx(out=cd[:].bitcast(FP8X4), scales=sc[:], in_=grp[:])
-                            codes[k] = cd
-                            scales[k] = sc
-                            if last:
-                                for g in range(2 * SUP):
-                                    if k == 0:
-                                        acc = ps.tile([P, 2 * O], F32, name="acc", tag=LAST_TAGS[g][0], bufs=LAST_TAGS[g][1])
-                                        accs.append(acc)
-                                    mx_pass(accs[g], cd, sc, g // 2, g % 2, k)
+                            gap()
+                            defer(st, k, planes[k], rt)
 
                     if c == 0:
                         prepare_bias()
                         prepare_coef()
-                    for s in range(SUP):
-                        if not last:
-                            base_part(s)
-                        for q in range(2):
-                            if last:
-                                acc = accs[2 * s + q]
-                            else:
-                                acc = ps.tile([P, 2 * O], F32, name="acc", tag="bank", bufs=5)
-                                for k in range(NC):
-                                    mx_pass(acc, codes[k], scales[k], s, q, k)
-                            close(s, q, acc)
+
+                for n in range(len(pending) - issued[0]):
+                    gap()

@@ -20,7 +20,7 @@ NCH = ROWS // CH_ROWS
 W = SUP * P
 NKN = 12
 LAST_TAGS = (("bank", 5),) * 5 + (("psx", 2),) * 2 + (("psb", 1),)
-ACT_REGROUP = (0, 1, 3, 4, 6)
+ACT_REGROUP = (0, 1, 3, 4, 6, 7)
 
 
 def tile_kanlinear_t_kernel(tc, x, grid, coef, base_weight, base_bias, out):
@@ -259,15 +259,16 @@ def tile_kanlinear_t_kernel(tc, x, grid, coef, base_weight, base_bias, out):
                         .bitcast(F32)
                         .rearrange("p (s m u) -> p s m u", s=SUP, m=P, u=2)
                     )
-                    xp = io.tile([P, 4, W], BF16, tag="xp", bufs=2)
+                    xwords = io.tile([P, 2, W], F32, tag="xwords", bufs=2)
+                    xp = []
                     for u in range(2):
                         psx = ps.tile([P, W], F32, name="psx", tag="psx", bufs=2)
                         for s in range(SUP):
                             nc.tensor.transpose(psx[:, s * P : (s + 1) * P], xw[:, s, :, u], ident_f[:])
-                        nc.scalar.copy(
-                            out=xp[:, 2 * u : 2 * u + 2, :],
-                            in_=psx[:].bitcast(BF16).rearrange("p (c e) -> p e c", e=2),
-                        )
+                        nc.scalar.copy(out=xwords[:, u, :], in_=psx[:])
+                        pair = xwords[:, u, :].bitcast(BF16).rearrange("p (c e) -> p e c", e=2)
+                        for e in range(2):
+                            xp.append(pair[:, e, :])
                     xT = io.tile([P, CH_ROWS * P], BF16, tag="xT", bufs=2)
                     for half in range(CH_ROWS // 8):
                         psb = ps.tile([P, 8 * P], BF16, name="psb", tag="psb", bufs=1)
@@ -285,10 +286,10 @@ def tile_kanlinear_t_kernel(tc, x, grid, coef, base_weight, base_bias, out):
                         has_left = 1 <= j <= 8
                         for t in range(4):
                             sq = work.tile([P, W], F32, tag="sq", bufs=6)
-                            nc.scalar.activation(out=sq[:], in_=xp[:, t, :], func=AF.Square, bias=nk[:, t, j : j + 1], scale=1.0)
+                            nc.scalar.activation(out=sq[:], in_=xp[t], func=AF.Square, bias=nk[:, t, j : j + 1], scale=1.0)
                             cj = work.tile([P, W], F32, name="cj", tag="c%d" % t, bufs=3)
                             nc.vector.scalar_tensor_tensor(
-                                out=cj[:], in0=xp[:, t, :], scalar=kn[:, t, j : j + 1], in1=sq[:], op0=ALU.subtract, op1=ALU.mult
+                                out=cj[:], in0=xp[t], scalar=kn[:, t, j : j + 1], in1=sq[:], op0=ALU.subtract, op1=ALU.mult
                             )
                             cub[(j, t)] = cj
                             if t == 1 and not has_left:

@@ -39,7 +39,7 @@ def tile_kanlinear_t_kernel(tc, x, grid, coef, base_weight, base_bias, out):
         nb4 = const.tile([P, 4, NC], F32)
         nb3 = const.tile([P, 4, NC], F32)
         bw = const.tile([P, O], BF16)
-        bias2 = const.tile([P, 2, O], F32)
+        bias_f = const.tile([P, O], F32)
         rh = const.tile([P, NC, 2, 2 * O], U32, align_bytes=64)
         rhs_sc = const.tile([P, NC, 2, 2 * O], U8, align_bytes=64)
         nc.vector.memset(rh[:].rearrange("p k q w -> p (k q w)").bitcast(I32), 0)
@@ -48,15 +48,15 @@ def tile_kanlinear_t_kernel(tc, x, grid, coef, base_weight, base_bias, out):
         with tc.tile_pool(name="prep", bufs=1) as prep:
             g_bf = prep.tile([P, 24], BF16)
             gsrc = grid.rearrange("(j t) g -> j (t g)", t=4)
-            for r in range(4):
-                nc.sync.dma_start(out=g_bf[32 * r : 32 * r + 32, :], in_=gsrc)
+            for r4 in range(4):
+                nc.sync.dma_start(out=g_bf[32 * r4 : 32 * r4 + 32, :], in_=gsrc)
             nc.scalar.dma_start(out=bw[:], in_=base_weight)
             bias_bf = prep.tile([P, O], BF16)
             nc.scalar.dma_start(out=bias_bf[:], in_=base_bias.partition_broadcast(P))
             craw = prep.tile([P, 4 * O * NC], BF16)
             csrc = coef.rearrange("(j t) o k -> j (t o k)", t=4)
-            for r in range(4):
-                nc.scalar.dma_start(out=craw[32 * r : 32 * r + 32, :], in_=csrc)
+            for r4 in range(4):
+                nc.scalar.dma_start(out=craw[32 * r4 : 32 * r4 + 32, :], in_=csrc)
 
             nc.vector.tensor_copy(out=kn[:, :, 3:9], in_=g_bf[:].rearrange("p (t g) -> p t g", g=6))
             five = prep.tile([P, 1], F32)
@@ -102,8 +102,7 @@ def tile_kanlinear_t_kernel(tc, x, grid, coef, base_weight, base_bias, out):
             nc.vector.tensor_tensor(out=den3[:], in0=den3[:], in1=d4[:], op=ALU.mult)
             nc.vector.tensor_scalar(out=nb3[:], in0=den3[:], scalar1=-1.0, scalar2=None, op0=ALU.mult)
 
-            for h in range(2):
-                nc.vector.tensor_copy(out=bias2[:, h, :], in_=bias_bf[:])
+            nc.vector.tensor_copy(out=bias_f[:], in_=bias_bf[:])
 
             def prepare_coef():
                 cv = craw[:].rearrange("p (t o k) -> p t o k", t=4, o=O, k=NC)
@@ -117,9 +116,9 @@ def tile_kanlinear_t_kernel(tc, x, grid, coef, base_weight, base_bias, out):
                         scales=sall[:, k, :],
                         in_=cg[:].rearrange("p o t -> p (o t)"),
                     )
-                for r in range(4):
-                    q, h = r // 2, r % 2
-                    rows = slice(32 * r, 32 * r + 32)
+                for r4 in range(4):
+                    q, h = r4 // 2, r4 % 2
+                    rows = slice(32 * r4, 32 * r4 + 32)
                     nc.vector.tensor_copy(
                         out=rh[rows, :, q, h * O : (h + 1) * O].bitcast(I32),
                         in_=call[rows, :, :].bitcast(I32),
@@ -129,7 +128,6 @@ def tile_kanlinear_t_kernel(tc, x, grid, coef, base_weight, base_bias, out):
                         in_=sall[rows, :, :].bitcast(I32),
                     )
 
-
             with tc.tile_pool(name="io", bufs=2) as io, tc.tile_pool(name="work", bufs=2) as work, tc.tile_pool(
                 name="mxop", bufs=1
             ) as mxop, tc.psum_pool(name="ps", bufs=1) as ps:
@@ -138,9 +136,8 @@ def tile_kanlinear_t_kernel(tc, x, grid, coef, base_weight, base_bias, out):
                 def prepare_bias():
                     for h in range(2):
                         pbt = ps.tile([P, P], F32, name="pbt", tag="psx", bufs=2)
-                        nc.tensor.transpose(pbt[:], bias2[:, 0, h * P : (h + 1) * P], ident_f[:])
+                        nc.tensor.transpose(pbt[:], bias_f[:, h * P : (h + 1) * P], ident_f[:])
                         nc.vector.tensor_copy(out=bias_t[:, h, :], in_=pbt[:])
-
 
                 def mx_pass(acc, cd, sc, s, q, k):
                     nc.tensor.matmul_mx(

import concourse.mybir as mybir
from concourse.masks import make_identity

F32 = mybir.dt.float32
BF16 = mybir.dt.bfloat16
U32 = mybir.dt.uint32
U8 = mybir.dt.uint8
I32 = mybir.dt.int32
FP8X4 = mybir.dt.float8_e4m3fn_x4
ALU = mybir.AluOpType
AF = mybir.ActivationFunctionType

B, I, O, NC = 16384, 128, 256, 8
FLOPS = 2 * B * (NC * I + I) * O
P = 128
ROWS = B // P
SUP = 4
CH_ROWS = 4 * SUP
NCH = ROWS // CH_ROWS
W = SUP * P
NKN = 12
LAST_TAGS = (("bank", 5),) * 5 + (("psx", 2),) * 2 + (("psb", 1),)
ACT_REGROUP = (0, 1, 3, 4, 6, 7)


def tile_kanlinear_t_kernel(tc, x, grid, coef, base_weight, base_bias, out):
    nc = tc.nc
    xv = x.rearrange("(n r) i -> n r i", r=ROWS)
    ov = out.rearrange("(n r) o -> n r o", r=ROWS)
    with tc.tile_pool(name="const", bufs=1) as const:
        ident_f = const.tile([P, P], F32)
        make_identity(nc, ident_f[:])
        ident_b = const.tile([P, P], BF16)
        make_identity(nc, ident_b[:])
        kn = const.tile([P, 4, NKN], F32)
        nk = const.tile([P, 4, NKN], F32)
        a0 = const.tile([P, 4, NC], F32)
        a1 = const.tile([P, 4, NC], F32)
        nb4 = const.tile([P, 4, NC], F32)
        nb3 = const.tile([P, 4, NC], F32)
        bw = const.tile([P, O], BF16)
        bias_f = const.tile([P, O], F32)
        rh = const.tile([P, NC, 2, 2 * O], U32, align_bytes=64)
        rhs_sc = const.tile([P, NC, 2, 2 * O], U8, align_bytes=64)
        nc.vector.memset(rh[:].rearrange("p k q w -> p (k q w)").bitcast(I32), 0)
        nc.vector.memset(rhs_sc[:].rearrange("p k q w -> p (k q w)").bitcast(I32), 0)

        with tc.tile_pool(name="prep", bufs=1) as prep:
            g_bf = prep.tile([P, 24], BF16)
            gsrc = grid.rearrange("(j t) g -> j (t g)", t=4)
            for r4 in range(4):
                nc.sync.dma_start(out=g_bf[32 * r4 : 32 * r4 + 32, :], in_=gsrc)
            nc.scalar.dma_start(out=bw[:], in_=base_weight)
            bias_bf = prep.tile([P, O], BF16)
            nc.scalar.dma_start(out=bias_bf[:], in_=base_bias.partition_broadcast(P))
            craw = prep.tile([P, 4 * O * NC], BF16)
            csrc = coef.rearrange("(j t) o k -> j (t o k)", t=4)
            for r4 in range(4):
                nc.scalar.dma_start(out=craw[32 * r4 : 32 * r4 + 32, :], in_=csrc)

            nc.vector.tensor_copy(out=kn[:, :, 3:9], in_=g_bf[:].rearrange("p (t g) -> p t g", g=6))
            five = prep.tile([P, 1], F32)
            nc.vector.memset(five[:], 5.0)
            fifth = prep.tile([P, 1], F32)
            nc.vector.reciprocal(out=fifth[:], in_=five[:])
            hh = prep.tile([P, 4, 1], F32)
            nc.vector.tensor_tensor(out=hh[:], in0=kn[:, :, 8:9], in1=kn[:, :, 3:4], op=ALU.subtract)
            nc.vector.tensor_scalar(out=hh[:], in0=hh[:], scalar1=fifth[:, 0:1], scalar2=None, op0=ALU.mult)
            for m in (2, 1, 0):
                nc.vector.tensor_tensor(out=kn[:, :, m : m + 1], in0=kn[:, :, m + 1 : m + 2], in1=hh[:], op=ALU.subtract)
            for m in (9, 10, 11):
                nc.vector.tensor_tensor(out=kn[:, :, m : m + 1], in0=kn[:, :, m - 1 : m], in1=hh[:], op=ALU.add)
            nc.vector.tensor_scalar(out=nk[:], in0=kn[:], scalar1=-1.0, scalar2=None, op0=ALU.mult)
            d1 = prep.tile([P, 4, 11], F32)
            d2 = prep.tile([P, 4, 10], F32)
            d3 = prep.tile([P, 4, 9], F32)
            d4 = prep.tile([P, 4, 8], F32)
            nc.vector.tensor_tensor(out=d1[:], in0=kn[:, :, 1:12], in1=kn[:, :, 0:11], op=ALU.subtract)
            nc.vector.tensor_tensor(out=d2[:], in0=kn[:, :, 2:12], in1=kn[:, :, 0:10], op=ALU.subtract)
            nc.vector.tensor_tensor(out=d3[:], in0=kn[:, :, 3:12], in1=kn[:, :, 0:9], op=ALU.subtract)
            nc.vector.tensor_tensor(out=d4[:], in0=kn[:, :, 4:12], in1=kn[:, :, 0:8], op=ALU.subtract)

            def product(dst, factors):
                nc.vector.tensor_tensor(out=dst[:], in0=factors[0], in1=factors[1], op=ALU.mult)
                for f in factors[2:]:
                    nc.vector.tensor_tensor(out=dst[:], in0=dst[:], in1=f, op=ALU.mult)

            den0 = prep.tile([P, 4, NC], F32)
            product(den0, [d1[:, :, 0:8], d2[:, :, 0:8], d3[:, :, 0:8]])
            nc.vector.reciprocal(out=a0[:], in_=den0[:])
            den1 = prep.tile([P, 4, NC], F32)
            product(den1, [d1[:, :, 0:8], d1[:, :, 1:9], d2[:, :, 1:9], d3[:, :, 1:9]])
            nc.vector.reciprocal(out=den1[:], in_=den1[:])
            nc.vector.tensor_tensor(out=a1[:], in0=den1[:], in1=d4[:], op=ALU.mult)
            den4 = prep.tile([P, 4, NC], F32)
            product(den4, [d3[:, :, 1:9], d2[:, :, 2:10], d1[:, :, 3:11]])
            nc.vector.reciprocal(out=den4[:], in_=den4[:])
            nc.vector.tensor_scalar(out=nb4[:], in0=den4[:], scalar1=-1.0, scalar2=None, op0=ALU.mult)
            den3 = prep.tile([P, 4, NC], F32)
            product(den3, [d3[:, :, 0:8], d2[:, :, 1:9], d1[:, :, 2:10], d1[:, :, 3:11]])
            nc.vector.reciprocal(out=den3[:], in_=den3[:])
            nc.vector.tensor_tensor(out=den3[:], in0=den3[:], in1=d4[:], op=ALU.mult)
            nc.vector.tensor_scalar(out=nb3[:], in0=den3[:], scalar1=-1.0, scalar2=None, op0=ALU.mult)

            nc.vector.tensor_copy(out=bias_f[:], in_=bias_bf[:])

            def prepare_coef():
                cv = craw[:].rearrange("p (t o k) -> p t o k", t=4, o=O, k=NC)
                call = prep.tile([P, NC, O], U32, align_bytes=64)
                sall = prep.tile([P, NC, O], U8, align_bytes=64)
                for k in range(NC):
                    cg = prep.tile([P, O, 4], BF16, align_bytes=64, tag="cg", bufs=2)
                    nc.scalar.copy(out=cg[:], in_=cv[:, :, :, k].rearrange("p t o -> p o t"))
                    nc.vector.quantize_mx(
                        out=call[:, k, :].bitcast(FP8X4),
                        scales=sall[:, k, :],
                        in_=cg[:].rearrange("p o t -> p (o t)"),
                    )
                for r4 in range(4):
                    q, h = r4 // 2, r4 % 2
                    rows = slice(32 * r4, 32 * r4 + 32)
                    nc.vector.tensor_copy(
                        out=rh[rows, :, q, h * O : (h + 1) * O].bitcast(I32),
                        in_=call[rows, :, :].bitcast(I32),
                    )
                    nc.vector.tensor_copy(
                        out=rhs_sc[rows, :, q, h * O : (h + 1) * O].bitcast(I32),
                        in_=sall[rows, :, :].bitcast(I32),
                    )

            with tc.tile_pool(name="io", bufs=2) as io, tc.tile_pool(name="work", bufs=2) as work, tc.tile_pool(
                name="mxop", bufs=1
            ) as mxop, tc.psum_pool(name="ps", bufs=1) as ps:
                bias_t = const.tile([P, 2, P], F32)

                def prepare_bias():
                    for h in range(2):
                        pbt = ps.tile([P, P], F32, name="pbt", tag="psx", bufs=2)
                        nc.tensor.transpose(pbt[:], bias_f[:, h * P : (h + 1) * P], ident_f[:])
                        nc.vector.tensor_copy(out=bias_t[:, h, :], in_=pbt[:])

                def mx_pass(acc, cd, sc, s, q, k):
                    nc.tensor.matmul_mx(
                        out=acc[:],
                        lhsT=cd[:, s * P : (s + 1) * P].bitcast(FP8X4),
                        lhsT_scale=sc[:, s * P : (s + 1) * P],
                        rhs=rh[:, k, q, :].bitcast(FP8X4),
                        rhs_scale=rhs_sc[:, k, q, :],
                        start=(k == 0),
                        stop=(k == NC - 1),
                    )

                pending = []
                issued = [0]

                def gap():
                    if issued[0] < len(pending):
                        op = pending[issued[0]]
                        issued[0] += 1
                        op()

                def base_part(st, s):
                    osb = io.tile([P, 4 * O], F32, name="osb", tag="osb", bufs=4)
                    st["outs"].append(osb)
                    xT = st["xT"]
                    for q in range(2):
                        psbase = ps.tile([P, 2 * O], F32, name="psbase", tag="bank", bufs=5)
                        for w in range(4):
                            nc.tensor.matmul(
                                out=psbase[:, w * P : (w + 1) * P],
                                lhsT=bias_t[:, w % 2, :],
                                rhs=ident_f[:],
                                is_transpose=True,
                                start=(w == 0),
                                stop=False,
                            )
                        for h in range(2):
                            row = 4 * s + 2 * q + h
                            nc.tensor.matmul(
                                out=psbase[:, h * O : (h + 1) * O],
                                lhsT=xT[:, row * P : (row + 1) * P],
                                rhs=bw[:],
                                start=False,
                                stop=(h == 1),
                            )
                        nc.scalar.copy(out=osb[:, q * 2 * O : (q + 1) * 2 * O], in_=psbase[:])

                def close(st, s, q, acc):
                    part = st["outs"][s][:, q * 2 * O : (q + 1) * 2 * O]
                    nc.vector.tensor_tensor(out=part, in0=acc[:], in1=part, op=ALU.add)
                    if q == 1:
                        r0 = st["c"] * CH_ROWS + 4 * s
                        nc.sync.dma_start(
                            out=ov[:, r0 : r0 + 4, :], in_=st["outs"][s][:].rearrange("p (r o) -> p r o", o=O)
                        )

                def max_op(npl, rt):
                    return lambda: nc.vector.tensor_tensor(out=npl[:], in0=npl[:], in1=rt[:], op=ALU.max)

                def regroup(st, k, npl):
                    grp = work.tile([P, 4 * W], BF16, name="grp", tag="grp", bufs=2, align_bytes=64)
                    st["grp"][k] = grp
                    gdst = grp[:].rearrange("p (c i t) -> p c t i", i=4, t=4)
                    gsrc2 = npl[:].rearrange("p t (c i) -> p c t i", i=4)
                    if k in ACT_REGROUP:
                        nc.scalar.activation(out=gdst, in_=gsrc2, func=AF.Relu)
                    else:
                        nc.vector.tensor_scalar(out=gdst, in0=gsrc2, scalar1=0.0, scalar2=None, op0=ALU.max)

                def quantise(st, k):
                    cd = mxop.tile([P, W], U32, name="cd", tag="cd%d" % k, bufs=1, align_bytes=64)
                    sc = mxop.tile([P, W], U8, name="sc", tag="sc%d" % k, bufs=1, align_bytes=64)
                    nc.vector.quantize_mx(out=cd[:].bitcast(FP8X4), scales=sc[:], in_=st["grp"][k][:])
                    st["codes"][k] = cd
                    st["scales"][k] = sc
                    if st["last"]:
                        for g in range(2 * SUP):
                            if k == 0:
                                acc = ps.tile([P, 2 * O], F32, name="acc", tag=LAST_TAGS[g][0], bufs=LAST_TAGS[g][1])
                                st["accs"].append(acc)
                            mx_pass(st["accs"][g], cd, sc, g // 2, g % 2, k)

                def finish(st):
                    for s in range(SUP):
                        if not st["last"]:
                            base_part(st, s)
                        for q in range(2):
                            if st["last"]:
                                acc = st["accs"][2 * s + q]
                            else:
                                acc = ps.tile([P, 2 * O], F32, name="acc", tag="bank", bufs=5)
                                for k in range(NC):
                                    mx_pass(acc, st["codes"][k], st["scales"][k], s, q, k)
                            close(st, s, q, acc)

                def all_bases(st):
                    def run():
                        for s in range(SUP):
                            base_part(st, s)

                    return run

                def defer(st, k, npl, rt):
                    pending.append(max_op(npl, rt))
                    pending.append(lambda: regroup(st, k, npl))
                    pending.append(lambda: quantise(st, k))
                    if k == NC - 1:
                        pending.append(lambda: finish(st))

                for c in range(NCH):
                    xraw = io.tile([P, CH_ROWS, I], BF16, tag="xraw", bufs=2)
                    nc.sync.dma_start(out=xraw[:], in_=xv[:, c * CH_ROWS : (c + 1) * CH_ROWS, :])
                    xw = (
                        xraw[:]
                        .rearrange("p r i -> p (r i)")
                        .bitcast(F32)
                        .rearrange("p (s m u) -> p s m u", s=SUP, m=P, u=2)
                    )
                    xwords = io.tile([P, 2, W], F32, tag="xwords", bufs=2)
                    xp = []
                    for u in range(2):
                        psx = ps.tile([P, W], F32, name="psx", tag="psx", bufs=2)
                        for s in range(SUP):
                            nc.tensor.transpose(psx[:, s * P : (s + 1) * P], xw[:, s, :, u], ident_f[:])
                        nc.scalar.copy(out=xwords[:, u, :], in_=psx[:])
                        pair = xwords[:, u, :].bitcast(BF16).rearrange("p (c e) -> p e c", e=2)
                        for e in range(2):
                            xp.append(pair[:, e, :])
                    xT = io.tile([P, CH_ROWS * P], BF16, tag="xT", bufs=2)
                    for half in range(CH_ROWS // 8):
                        psb = ps.tile([P, 8 * P], BF16, name="psb", tag="psb", bufs=1)
                        for rr in range(8):
                            nc.tensor.transpose(psb[:, rr * P : (rr + 1) * P], xraw[:, half * 8 + rr, :], ident_b[:])
                        nc.scalar.copy(out=xT[:, half * 8 * P : (half + 1) * 8 * P], in_=psb[:])

                    st = {"c": c, "last": c == NCH - 1, "xT": xT, "outs": [], "accs": [], "codes": {}, "scales": {}, "grp": {}}
                    if st["last"]:
                        pending.append(all_bases(st))

                    cub = {}
                    planes = {}
                    for j in range(NKN):
                        has_left = 1 <= j <= 8
                        for t in range(4):
                            sq = work.tile([P, W], F32, tag="sq", bufs=6)
                            nc.scalar.activation(out=sq[:], in_=xp[t], func=AF.Square, bias=nk[:, t, j : j + 1], scale=1.0)
                            cj = work.tile([P, W], F32, name="cj", tag="c%d" % t, bufs=3)
                            nc.vector.scalar_tensor_tensor(
                                out=cj[:], in0=xp[t], scalar=kn[:, t, j : j + 1], in1=sq[:], op0=ALU.subtract, op1=ALU.mult
                            )
                            cub[(j, t)] = cj
                            if t == 1 and not has_left:
                                gap()
                        gap()
                        if has_left:
                            k = j - 1
                            npl = work.tile([P, 4, W], BF16, tag="npl", bufs=6)
                            planes[k] = npl
                            for t in range(4):
                                uu = work.tile([P, W], F32, tag="uu", bufs=8)
                                nc.scalar.activation(out=uu[:], in_=cub[(j, t)][:], func=AF.Relu, scale=a1[:, t, k : k + 1])
                                nc.vector.scalar_tensor_tensor(
                                    out=npl[:, t, :], in0=cub[(j - 1, t)][:], scalar=a0[:, t, k : k + 1], in1=uu[:], op0=ALU.mult, op1=ALU.subtract
                                )
                            gap()
                        if j >= 4:
                            k = j - 4
                            rt = work.tile([P, 4, W], BF16, tag="rt", bufs=3)
                            for t in range(4):
                                vv = work.tile([P, W], F32, name="vv", tag="uu", bufs=8)
                                nc.scalar.activation(out=vv[:], in_=cub[(j - 1, t)][:], func=AF.Relu, scale=nb3[:, t, k : k + 1])
                                nc.vector.scalar_tensor_tensor(
                                    out=rt[:, t, :], in0=cub[(j, t)][:], scalar=nb4[:, t, k : k + 1], in1=vv[:], op0=ALU.mult, op1=ALU.subtract
                                )
                            gap()
                            defer(st, k, planes[k], rt)

                    if c == 0:
                        prepare_bias()
                        prepare_coef()

                for n in range(len(pending) - issued[0]):
                    gap()
